import numpy as np
import ml_dtypes


def mxq(x, axis, fmt="e4m3"):
    dtype, down = {"e4m3": (ml_dtypes.float8_e4m3fn, 7), "e5m2": (ml_dtypes.float8_e5m2, 14)}[fmt]
    v = np.moveaxis(np.asarray(x, np.float32).astype(ml_dtypes.bfloat16).astype(np.float64), axis, -1)
    blocks = v.reshape(v.shape[:-1] + (-1, 32))
    amax = np.abs(blocks).max(-1, keepdims=True)
    byte = np.maximum(np.where(amax > 0, np.frexp(amax)[1] - 1 + 127, 0) - down, 1)
    scale = np.exp2(byte - 127.0)
    codes = (blocks / scale).astype(np.float32).astype(dtype).astype(np.float64)
    return np.moveaxis((codes * scale).reshape(v.shape), -1, axis)


WIDE = False


def mx_kscale(k):
    if not WIDE:
        return np.ones(k)
    levels = np.array([10, -10, 5, -5, 0])
    a = np.random.permutation(np.resize(levels, k // 512 * 4)).reshape(k // 512, 4)
    idx = np.arange(k)
    return np.exp2(a[idx // 512, idx % 128 // 32])


BF16 = ml_dtypes.bfloat16


def bf(x):
    return np.asarray(x, np.float32).astype(BF16)


def f64(x):
    return np.asarray(x).astype(np.float64)


B, S, E, R = 4, 1024, 512, 2
F = R * E
EPS = 1e-5


def layer_norm(y, g, b):
    mu = y.mean(-1, keepdims=True)
    var = np.square(y - mu).mean(-1, keepdims=True)
    return (y - mu) / np.sqrt(var + EPS) * g + b


def setup_inputs():
    t = mx_kscale(F)
    return {"x2": bf(np.random.standard_normal((B, S, E))),
            "mlp_w1": bf(np.random.standard_normal((E, F)) / np.sqrt(E) * t),
            "mlp_b1": bf(np.random.standard_normal(F) * 0.3 * t),
            "mlp_w2": bf(np.random.standard_normal((F, E)) * 1.5 / np.sqrt(F) / t[:, None]),
            "mlp_b2": bf(np.random.standard_normal(E) * 0.3),
            "ln3_g": bf(1.0 + 0.1 * np.random.standard_normal(E)),
            "ln3_b": bf(0.2 * np.random.standard_normal(E))}


def reference(x2, mlp_w1, mlp_b1, mlp_w2, mlp_b2, ln3_g, ln3_b):
    xf = f64(x2)
    h = np.maximum((mxq(xf, 2, "e4m3") @ mxq(f64(mlp_w1), 0, "e4m3")) + f64(mlp_b1), 0.0)
    m = np.maximum((mxq(h, 2, "e4m3") @ mxq(f64(mlp_w2), 0, "e4m3")) + f64(mlp_b2), 0.0)
    return layer_norm(xf + m, f64(ln3_g), f64(ln3_b))

@@ -1,0 +1,235 @@
+from contextlib import ExitStack
+
+import concourse.mybir as mybir
+from concourse.masks import make_identity
+
+F32 = mybir.dt.float32
+BF16 = mybir.dt.bfloat16
+U32 = mybir.dt.uint32
+U8 = mybir.dt.uint8
+FP8X4 = mybir.dt.float8_e4m3fn_x4
+ACT = mybir.ActivationFunctionType
+ALU = mybir.AluOpType
+
+P = 128
+PACK = 4
+K_PASS = P * PACK
+TOKENS = 4096
+E = 512
+F = 1024
+EPS = 1e-5
+GROUP = 512
+N_GROUPS = TOKENS // GROUP
+TILES = GROUP // P
+F_TILES = F // P
+E_TILES = E // P
+PASSES2 = F // K_PASS
+RUN = 4
+
+FLOPS = 2 * TOKENS * E * F * 2
+
+
+def interleave(nc, grouped, planes):
+    nc.vector.tensor_copy(
+        out=grouped.rearrange("p (c i) t -> p c t i", i=RUN),
+        in_=planes.rearrange("p t (c i) -> p c t i", i=RUN),
+    )
+
+
+def quantise(nc, codes, scales, grouped):
+    nc.vector.quantize_mx(
+        out=codes.bitcast(FP8X4),
+        scales=scales,
+        in_=grouped.rearrange("p c t -> p (c t)"),
+    )
+
+
+def tile_transformerdecoderblock_pb_t_kernel(
+    tc, x2, mlp_w1, mlp_b1, mlp_w2, mlp_b2, ln3_g, ln3_b, out
+):
+    nc = tc.nc
+    x_rows = x2.flatten_outer_dims().rearrange("(g p j) e -> g p j e", p=P, j=TILES)
+    out_rows = out.flatten_outer_dims().rearrange("(g p j) e -> g p j e", p=P, j=TILES)
+
+    with ExitStack() as stack:
+        keep = stack.enter_context(tc.tile_pool(name="keep", bufs=1))
+        work = stack.enter_context(tc.tile_pool(name="work", bufs=2))
+        psum = stack.enter_context(tc.psum_pool(name="psum", bufs=2))
+
+        x_sb = [keep.tile([P, TILES, E], BF16, name="x%d" % g) for g in range(N_GROUPS)]
+        w1_raw = keep.tile([P, PACK, F], BF16)
+        w2_raw = keep.tile([P, PASSES2 * PACK, E], BF16)
+        bias_rows = keep.tile([P, P], BF16)
+        gain = keep.tile([P, E], BF16)
+        shift = keep.tile([P, E], BF16)
+
+        halves = [slice(0, F // 2), slice(F // 2, F)]
+        nc.vector.memset(bias_rows[:], 0.0)
+        nc.sync.dma_start(out=x_sb[0][:], in_=x_rows[0])
+        nc.sync.dma_start(out=bias_rows[0:F_TILES, :], in_=mlp_b1.rearrange("(a p) -> a p", p=P))
+        nc.sync.dma_start(
+            out=bias_rows[F_TILES : F_TILES + E_TILES, :],
+            in_=mlp_b2.rearrange("(a p) -> a p", p=P),
+        )
+        for cols in halves:
+            for u in range(2):
+                nc.sync.dma_start(
+                    out=w1_raw[:, 2 * u : 2 * u + 2, cols],
+                    in_=mlp_w1[256 * u : 256 * (u + 1), cols].rearrange("(q e) f -> q e f", e=2),
+                )
+        nc.sync.dma_start(out=x_sb[1][:], in_=x_rows[1])
+        nc.sync.dma_start(out=w2_raw[:], in_=mlp_w2.rearrange("(a p) e -> p a e", p=P))
+        nc.sync.dma_start(out=gain[:], in_=ln3_g.partition_broadcast(P))
+        nc.sync.dma_start(out=shift[:], in_=ln3_b.partition_broadcast(P))
+        for g in range(2, N_GROUPS):
+            nc.sync.dma_start(out=x_sb[g][:], in_=x_rows[g])
+
+        ident_f32 = keep.tile([P, P], F32)
+        make_identity(nc, ident_f32[:])
+        ident_bf16 = keep.tile([P, P], BF16)
+        make_identity(nc, ident_bf16[:])
+        eps = keep.tile([P, 1], F32)
+        nc.vector.memset(eps[:], EPS)
+        table_warm = keep.tile([P, 1], F32)
+        nc.scalar.activation(out=table_warm[:], in_=eps[:], func=ACT.Sqrt)
+
+        bias_ps = psum.tile([P, P], BF16, tag="xt")
+        nc.tensor.transpose(bias_ps[:], bias_rows[:], ident_bf16[:])
+        bias_cols = keep.tile([P, F_TILES + E_TILES], F32)
+        nc.vector.tensor_copy(out=bias_cols[:], in_=bias_ps[:, 0 : F_TILES + E_TILES])
+
+        w1_grouped = keep.tile([P, F, PACK], BF16, align_bytes=64)
+        w1_codes = keep.tile([P, F], U32, align_bytes=64)
+        w1_scales = keep.tile([P, F], U8, align_bytes=64)
+        for cols in halves:
+            interleave(nc, w1_grouped[:, cols, :], w1_raw[:, :, cols])
+        for cols in halves:
+            quantise(nc, w1_codes[:, cols], w1_scales[:, cols], w1_grouped[:, cols, :])
+
+        w2_grouped = keep.tile([P, PASSES2, E, PACK], BF16, align_bytes=64)
+        w2_codes = keep.tile([P, PASSES2, E], U32, align_bytes=64)
+        w2_scales = keep.tile([P, PASSES2, E], U8, align_bytes=64)
+        for c in range(PASSES2):
+            interleave(nc, w2_grouped[:, c, :, :], w2_raw[:, c * PACK : (c + 1) * PACK, :])
+        for c in range(PASSES2):
+            quantise(nc, w2_codes[:, c, :], w2_scales[:, c, :], w2_grouped[:, c, :, :])
+
+        for g in range(N_GROUPS):
+            x_grouped = work.tile([P, GROUP, PACK], BF16, align_bytes=64)
+            x_words = (
+                x_grouped[:]
+                .rearrange("p c t -> p (c t)")
+                .bitcast(F32)
+                .rearrange("p (c u) -> p c u", u=2)
+            )
+            for half in range(2):
+                xt = psum.tile([P, 2, 2 * P], F32, tag="xt")
+                for jj in range(2):
+                    words = x_sb[g][:, 2 * half + jj, :].bitcast(F32)
+                    for u in range(2):
+                        nc.tensor.transpose(
+                            xt[:, u, jj * P : (jj + 1) * P],
+                            words[:, u * P : (u + 1) * P],
+                            ident_f32[:],
+                        )
+                nc.scalar.copy(
+                    out=x_words[:, half * 2 * P : (half + 1) * 2 * P, :],
+                    in_=xt[:].rearrange("p u c -> p c u"),
+                )
+            x_codes = work.tile([P, GROUP], U32, align_bytes=64)
+            x_scales = work.tile([P, GROUP], U8, align_bytes=64)
+            quantise(nc, x_codes[:], x_scales[:], x_grouped[:])
+
+            h_codes = work.tile([P, PASSES2, GROUP], U32, align_bytes=64)
+            h_scales = work.tile([P, PASSES2, GROUP], U8, align_bytes=64)
+            h_grouped = work.tile([P, PASSES2, GROUP, PACK], BF16, align_bytes=64)
+            for c in range(PASSES2):
+                h_planes = work.tile([P, PACK, GROUP], BF16)
+                for t in range(PACK):
+                    a = c * PACK + t
+                    h_ps = psum.tile([P, GROUP], F32, tag="h_ps")
+                    nc.tensor.matmul_mx(
+                        out=h_ps[:],
+                        lhsT=w1_codes[:, a * P : (a + 1) * P].bitcast(FP8X4),
+                        lhsT_scale=w1_scales[:, a * P : (a + 1) * P],
+                        rhs=x_codes[:].bitcast(FP8X4),
+                        rhs_scale=x_scales[:],
+                        start=True,
+                        stop=True,
+                    )
+                    nc.scalar.activation(
+                        out=h_planes[:, t, :],
+                        in_=h_ps[:],
+                        func=ACT.Relu,
+                        bias=bias_cols[:, a : a + 1],
+                        scale=1.0,
+                    )
+                interleave(nc, h_grouped[:, c, :, :], h_planes[:])
+            for c in range(PASSES2):
+                quantise(nc, h_codes[:, c, :], h_scales[:, c, :], h_grouped[:, c, :, :])
+
+            m_relu = work.tile([P, E_TILES, GROUP], F32)
+            for a in range(E_TILES):
+                m_ps = psum.tile([P, GROUP], F32, tag="m_ps")
+                for c in range(PASSES2):
+                    nc.tensor.matmul_mx(
+                        out=m_ps[:],
+                        lhsT=w2_codes[:, c, a * P : (a + 1) * P].bitcast(FP8X4),
+                        lhsT_scale=w2_scales[:, c, a * P : (a + 1) * P],
+                        rhs=h_codes[:, c, :].bitcast(FP8X4),
+                        rhs_scale=h_scales[:, c, :],
+                        start=(c == 0),
+                        stop=(c == PASSES2 - 1),
+                    )
+                nc.scalar.activation(
+                    out=m_relu[:, a, :],
+                    in_=m_ps[:],
+                    func=ACT.Relu,
+                    bias=bias_cols[:, F_TILES + a : F_TILES + a + 1],
+                    scale=1.0,
+                )
+
+            stats = work.tile([P, TILES, 6], F32)
+            mean_var = work.tile([P, TILES, 2], F32)
+            centred_gain = work.tile([P, TILES, E], F32)
+            for j in range(TILES):
+                y_ps = psum.tile([P, E], F32, tag="y_ps")
+                nc.tensor.matmul(
+                    out=y_ps[:], lhsT=ident_bf16[:], rhs=x_sb[g][:, j, :], start=True, stop=False
+                )
+                for a in range(E_TILES):
+                    nc.tensor.matmul(
+                        out=y_ps[:, a * P : (a + 1) * P],
+                        lhsT=m_relu[:, a, j * P : (j + 1) * P],
+                        rhs=ident_f32[:],
+                        is_transpose=True,
+                        start=False,
+                        stop=(a == E_TILES - 1),
+                    )
+                nc.vector.bn_stats(out=stats[:, j, :], in_=y_ps[:])
+                nc.vector.bn_aggr(out=mean_var[:, j, :], in_=stats[:, j, :])
+                nc.vector.scalar_tensor_tensor(
+                    out=centred_gain[:, j, :],
+                    in0=y_ps[:],
+                    scalar=mean_var[:, j, 0:1],
+                    in1=gain[:],
+                    op0=ALU.subtract,
+                    op1=ALU.mult,
+                )
+            std = work.tile([P, TILES], F32)
+            nc.scalar.activation(
+                out=std[:], in_=mean_var[:, :, 1], func=ACT.Sqrt, bias=eps[:], scale=1.0
+            )
+            rstd = work.tile([P, TILES], F32)
+            nc.vector.reciprocal(out=rstd[:], in_=std[:])
+            result = work.tile([P, TILES, E], F32)
+            for j in range(TILES):
+                nc.vector.scalar_tensor_tensor(
+                    out=result[:, j, :],
+                    in0=centred_gain[:, j, :],
+                    scalar=rstd[:, j : j + 1],
+                    in1=shift[:],
+                    op0=ALU.mult,
+                    op1=ALU.add,
+                )
+                nc.sync.dma_start(out=out_rows[g][:, j, :], in_=result[:, j, :])

@@ -36,6 +36,19 @@ def interleave(nc, grouped, planes):
     )
 
 
+def interleave_beside_vector(nc, grouped, planes):
+    for j in range(TILES):
+        cols = slice(j * P, (j + 1) * P)
+        nc.gpsimd.tensor_scalar(
+            out=grouped[:, cols, :],
+            in0=planes[:, :, cols].rearrange("p t c -> p c t"),
+            scalar1=1.0,
+            scalar2=0.0,
+            op0=ALU.mult,
+            op1=ALU.add,
+        )
+
+
 def quantise(nc, codes, scales, grouped):
     nc.vector.quantize_mx(
         out=codes.bitcast(FP8X4),
@@ -52,25 +65,28 @@ def tile_transformerdecoderblock_pb_t_kernel(
     out_rows = out.flatten_outer_dims().rearrange("(g p j) e -> g p j e", p=P, j=TILES)
 
     with ExitStack() as stack:
+        stack.enter_context(tc.manual_schedule())
         keep = stack.enter_context(tc.tile_pool(name="keep", bufs=1))
         work = stack.enter_context(tc.tile_pool(name="work", bufs=2))
-        psum = stack.enter_context(tc.psum_pool(name="psum", bufs=2))
+        psum = stack.enter_context(tc.psum_pool(name="psum", bufs=7))
 
         x_sb = [keep.tile([P, TILES, E], BF16, name="x%d" % g) for g in range(N_GROUPS)]
         w1_raw = keep.tile([P, PACK, F], BF16)
         w2_raw = keep.tile([P, PASSES2 * PACK, E], BF16)
         bias_rows = keep.tile([P, P], BF16)
+        shift_row = keep.tile([P, E], BF16)
         gain = keep.tile([P, E], BF16)
-        shift = keep.tile([P, E], BF16)
-
         halves = [slice(0, F // 2), slice(F // 2, F)]
+
         nc.vector.memset(bias_rows[:], 0.0)
+        nc.vector.memset(shift_row[:], 0.0)
         nc.sync.dma_start(out=x_sb[0][:], in_=x_rows[0])
         nc.sync.dma_start(out=bias_rows[0:F_TILES, :], in_=mlp_b1.rearrange("(a p) -> a p", p=P))
         nc.sync.dma_start(
             out=bias_rows[F_TILES : F_TILES + E_TILES, :],
             in_=mlp_b2.rearrange("(a p) -> a p", p=P),
         )
+        nc.sync.dma_start(out=shift_row[0:1, :], in_=ln3_b.rearrange("(o e) -> o e", o=1))
         for cols in halves:
             for u in range(2):
                 nc.sync.dma_start(
@@ -80,7 +96,6 @@ def tile_transformerdecoderblock_pb_t_kernel(
         nc.sync.dma_start(out=x_sb[1][:], in_=x_rows[1])
         nc.sync.dma_start(out=w2_raw[:], in_=mlp_w2.rearrange("(a p) e -> p a e", p=P))
         nc.sync.dma_start(out=gain[:], in_=ln3_g.partition_broadcast(P))
-        nc.sync.dma_start(out=shift[:], in_=ln3_b.partition_broadcast(P))
         for g in range(2, N_GROUPS):
             nc.sync.dma_start(out=x_sb[g][:], in_=x_rows[g])
 
@@ -88,148 +103,218 @@ def tile_transformerdecoderblock_pb_t_kernel(
         make_identity(nc, ident_f32[:])
         ident_bf16 = keep.tile([P, P], BF16)
         make_identity(nc, ident_bf16[:])
+        ones = keep.tile([P, P], BF16)
+        nc.vector.memset(ones[:], 1.0)
         eps = keep.tile([P, 1], F32)
         nc.vector.memset(eps[:], EPS)
         table_warm = keep.tile([P, 1], F32)
         nc.scalar.activation(out=table_warm[:], in_=eps[:], func=ACT.Sqrt)
 
-        bias_ps = psum.tile([P, P], BF16, tag="xt")
-        nc.tensor.transpose(bias_ps[:], bias_rows[:], ident_bf16[:])
-        bias_cols = keep.tile([P, F_TILES + E_TILES], F32)
-        nc.vector.tensor_copy(out=bias_cols[:], in_=bias_ps[:, 0 : F_TILES + E_TILES])
-
         w1_grouped = keep.tile([P, F, PACK], BF16, align_bytes=64)
         w1_codes = keep.tile([P, F], U32, align_bytes=64)
         w1_scales = keep.tile([P, F], U8, align_bytes=64)
-        for cols in halves:
-            interleave(nc, w1_grouped[:, cols, :], w1_raw[:, :, cols])
-        for cols in halves:
-            quantise(nc, w1_codes[:, cols], w1_scales[:, cols], w1_grouped[:, cols, :])
-
         w2_grouped = keep.tile([P, PASSES2, E, PACK], BF16, align_bytes=64)
         w2_codes = keep.tile([P, PASSES2, E], U32, align_bytes=64)
         w2_scales = keep.tile([P, PASSES2, E], U8, align_bytes=64)
+        bias_cols = keep.tile([P, F_TILES + E_TILES], F32)
+        shift_ps = psum.tile([P, E], F32, tag="shift_ps", bufs=1)
+
+        x_grouped, x_codes, x_scales = {}, {}, {}
+        h_planes, h_grouped, h_codes, h_scales = {}, {}, {}, {}
+        m_relu, y_ps, stats, mean_var, centred_gain, std, rstd = {}, {}, {}, {}, {}, {}, {}
+
+        def exists(g):
+            return 0 <= g < N_GROUPS
+
+        def transpose_x(g, half):
+            if not exists(g):
+                return
+            if half == 0:
+                x_grouped[g] = work.tile([P, GROUP, PACK], BF16, name="x_grouped", align_bytes=64)
+            x_words = (
+                x_grouped[g][:]
+                .rearrange("p c t -> p (c t)")
+                .bitcast(F32)
+                .rearrange("p (c u) -> p c u", u=2)
+            )
+            xt = psum.tile([P, 2, 2 * P], F32, tag="bank")
+            for jj in range(2):
+                words = x_sb[g][:, 2 * half + jj, :].bitcast(F32)
+                for u in range(2):
+                    nc.tensor.transpose(
+                        xt[:, u, jj * P : (jj + 1) * P], words[:, u * P : (u + 1) * P], ident_f32[:]
+                    )
+            nc.scalar.copy(
+                out=x_words[:, half * 2 * P : (half + 1) * 2 * P, :],
+                in_=xt[:].rearrange("p u c -> p c u"),
+            )
+
+        def quantise_x(g):
+            if not exists(g):
+                return
+            x_codes[g] = work.tile([P, GROUP], U32, name="x_codes", bufs=3, align_bytes=64)
+            x_scales[g] = work.tile([P, GROUP], U8, name="x_scales", bufs=3, align_bytes=64)
+            quantise(nc, x_codes[g][:], x_scales[g][:], x_grouped[g][:])
+
+        def first_matmul(g, a):
+            if not exists(g):
+                return
+            c, t = divmod(a, PACK)
+            if t == 0:
+                h_planes[g, c] = work.tile([P, PACK, GROUP], BF16, name="h_planes", bufs=4)
+            h_ps = psum.tile([P, GROUP], F32, tag="bank")
+            nc.tensor.matmul_mx(
+                out=h_ps[:],
+                lhsT=w1_codes[:, a * P : (a + 1) * P].bitcast(FP8X4),
+                lhsT_scale=w1_scales[:, a * P : (a + 1) * P],
+                rhs=x_codes[g][:].bitcast(FP8X4),
+                rhs_scale=x_scales[g][:],
+                start=True,
+                stop=True,
+            )
+            nc.scalar.activation(
+                out=h_planes[g, c][:, t, :],
+                in_=h_ps[:],
+                func=ACT.Relu,
+                bias=bias_cols[:, a : a + 1],
+                scale=1.0,
+            )
+
+        def interleave_h(g, c):
+            if not exists(g):
+                return
+            if c == 0:
+                h_grouped[g] = work.tile(
+                    [P, PASSES2, GROUP, PACK], BF16, name="h_grouped", align_bytes=64
+                )
+            interleave_beside_vector(nc, h_grouped[g][:, c, :, :], h_planes[g, c][:])
+
+        def quantise_h(g, c):
+            if not exists(g):
+                return
+            if c == 0:
+                h_codes[g] = work.tile([P, PASSES2, GROUP], U32, name="h_codes", align_bytes=64)
+                h_scales[g] = work.tile([P, PASSES2, GROUP], U8, name="h_scales", align_bytes=64)
+            quantise(nc, h_codes[g][:, c, :], h_scales[g][:, c, :], h_grouped[g][:, c, :, :])
+
+        def second_matmul(g, a):
+            if not exists(g):
+                return
+            if a == 0:
+                m_relu[g] = work.tile([P, E_TILES, GROUP], F32, name="m_relu")
+            m_ps = psum.tile([P, GROUP], F32, tag="bank")
+            for c in range(PASSES2):
+                nc.tensor.matmul_mx(
+                    out=m_ps[:],
+                    lhsT=w2_codes[:, c, a * P : (a + 1) * P].bitcast(FP8X4),
+                    lhsT_scale=w2_scales[:, c, a * P : (a + 1) * P],
+                    rhs=h_codes[g][:, c, :].bitcast(FP8X4),
+                    rhs_scale=h_scales[g][:, c, :],
+                    start=(c == 0),
+                    stop=(c == PASSES2 - 1),
+                )
+            nc.scalar.activation(
+                out=m_relu[g][:, a, :],
+                in_=m_ps[:],
+                func=ACT.Relu,
+                bias=bias_cols[:, F_TILES + a : F_TILES + a + 1],
+                scale=1.0,
+            )
+
+        def assemble_y(g, j):
+            if not exists(g):
+                return
+            y_ps[g, j] = psum.tile([P, E], F32, name="y_ps", tag="bank")
+            nc.tensor.matmul(
+                out=y_ps[g, j][:], lhsT=ident_bf16[:], rhs=x_sb[g][:, j, :], start=True, stop=False
+            )
+            for a in range(E_TILES):
+                nc.tensor.matmul(
+                    out=y_ps[g, j][:, a * P : (a + 1) * P],
+                    lhsT=m_relu[g][:, a, j * P : (j + 1) * P],
+                    rhs=ident_f32[:],
+                    is_transpose=True,
+                    start=False,
+                    stop=(a == E_TILES - 1),
+                )
+
+        def centre_and_gain(g, j):
+            if not exists(g):
+                return
+            if j == 0:
+                stats[g] = work.tile([P, TILES, 6], F32, name="stats")
+                mean_var[g] = work.tile([P, TILES, 2], F32, name="mean_var")
+                centred_gain[g] = work.tile([P, TILES, E], F32, name="centred_gain")
+            nc.vector.bn_stats(out=stats[g][:, j, :], in_=y_ps[g, j][:])
+            nc.vector.bn_aggr(out=mean_var[g][:, j, :], in_=stats[g][:, j, :])
+            nc.vector.scalar_tensor_tensor(
+                out=centred_gain[g][:, j, :],
+                in0=y_ps[g, j][:],
+                scalar=mean_var[g][:, j, 0:1],
+                in1=gain[:],
+                op0=ALU.subtract,
+                op1=ALU.mult,
+            )
+
+        def standard_deviation(g):
+            if not exists(g):
+                return
+            std[g] = work.tile([P, TILES], F32, name="std")
+            nc.scalar.activation(
+                out=std[g][:], in_=mean_var[g][:, :, 1], func=ACT.Sqrt, bias=eps[:], scale=1.0
+            )
+
+        def scale_shift_store(g):
+            if not exists(g):
+                return
+            rstd[g] = work.tile([P, TILES], F32, name="rstd")
+            nc.vector.reciprocal(out=rstd[g][:], in_=std[g][:])
+            for j in range(TILES):
+                result = work.tile([P, E], F32, bufs=4)
+                nc.vector.scalar_tensor_tensor(
+                    out=result[:],
+                    in0=centred_gain[g][:, j, :],
+                    scalar=rstd[g][:, j : j + 1],
+                    in1=shift_ps[:],
+                    op0=ALU.mult,
+                    op1=ALU.add,
+                )
+                nc.sync.dma_start(out=out_rows[g][:, j, :], in_=result[:])
+
+        transpose_x(0, 0)
+        transpose_x(0, 1)
+        bias_ps = psum.tile([P, P], BF16, tag="bank")
+        nc.tensor.transpose(bias_ps[:], bias_rows[:], ident_bf16[:])
+        nc.vector.tensor_copy(out=bias_cols[:], in_=bias_ps[:, 0 : F_TILES + E_TILES])
+        nc.tensor.matmul(out=shift_ps[:], lhsT=ones[:], rhs=shift_row[:], start=True, stop=True)
+        transpose_x(1, 0)
+        transpose_x(1, 1)
+
+        interleave(nc, w1_grouped[:, halves[0], :], w1_raw[:, :, halves[0]])
+        quantise_x(0)
+        quantise(nc, w1_codes[:, halves[0]], w1_scales[:, halves[0]], w1_grouped[:, halves[0], :])
+        interleave(nc, w1_grouped[:, halves[1], :], w1_raw[:, :, halves[1]])
+        quantise(nc, w1_codes[:, halves[1]], w1_scales[:, halves[1]], w1_grouped[:, halves[1], :])
+        quantise_x(1)
         for c in range(PASSES2):
             interleave(nc, w2_grouped[:, c, :, :], w2_raw[:, c * PACK : (c + 1) * PACK, :])
         for c in range(PASSES2):
             quantise(nc, w2_codes[:, c, :], w2_scales[:, c, :], w2_grouped[:, c, :, :])
 
-        for g in range(N_GROUPS):
-            x_grouped = work.tile([P, GROUP, PACK], BF16, align_bytes=64)
-            x_words = (
-                x_grouped[:]
-                .rearrange("p c t -> p (c t)")
-                .bitcast(F32)
-                .rearrange("p (c u) -> p c u", u=2)
-            )
-            for half in range(2):
-                xt = psum.tile([P, 2, 2 * P], F32, tag="xt")
-                for jj in range(2):
-                    words = x_sb[g][:, 2 * half + jj, :].bitcast(F32)
-                    for u in range(2):
-                        nc.tensor.transpose(
-                            xt[:, u, jj * P : (jj + 1) * P],
-                            words[:, u * P : (u + 1) * P],
-                            ident_f32[:],
-                        )
-                nc.scalar.copy(
-                    out=x_words[:, half * 2 * P : (half + 1) * 2 * P, :],
-                    in_=xt[:].rearrange("p u c -> p c u"),
-                )
-            x_codes = work.tile([P, GROUP], U32, align_bytes=64)
-            x_scales = work.tile([P, GROUP], U8, align_bytes=64)
-            quantise(nc, x_codes[:], x_scales[:], x_grouped[:])
-
-            h_codes = work.tile([P, PASSES2, GROUP], U32, align_bytes=64)
-            h_scales = work.tile([P, PASSES2, GROUP], U8, align_bytes=64)
-            h_grouped = work.tile([P, PASSES2, GROUP, PACK], BF16, align_bytes=64)
-            for c in range(PASSES2):
-                h_planes = work.tile([P, PACK, GROUP], BF16)
-                for t in range(PACK):
-                    a = c * PACK + t
-                    h_ps = psum.tile([P, GROUP], F32, tag="h_ps")
-                    nc.tensor.matmul_mx(
-                        out=h_ps[:],
-                        lhsT=w1_codes[:, a * P : (a + 1) * P].bitcast(FP8X4),
-                        lhsT_scale=w1_scales[:, a * P : (a + 1) * P],
-                        rhs=x_codes[:].bitcast(FP8X4),
-                        rhs_scale=x_scales[:],
-                        start=True,
-                        stop=True,
-                    )
-                    nc.scalar.activation(
-                        out=h_planes[:, t, :],
-                        in_=h_ps[:],
-                        func=ACT.Relu,
-                        bias=bias_cols[:, a : a + 1],
-                        scale=1.0,
-                    )
-                interleave(nc, h_grouped[:, c, :, :], h_planes[:])
-            for c in range(PASSES2):
-                quantise(nc, h_codes[:, c, :], h_scales[:, c, :], h_grouped[:, c, :, :])
-
-            m_relu = work.tile([P, E_TILES, GROUP], F32)
+        for f in range(-2, N_GROUPS + 1):
             for a in range(E_TILES):
-                m_ps = psum.tile([P, GROUP], F32, tag="m_ps")
-                for c in range(PASSES2):
-                    nc.tensor.matmul_mx(
-                        out=m_ps[:],
-                        lhsT=w2_codes[:, c, a * P : (a + 1) * P].bitcast(FP8X4),
-                        lhsT_scale=w2_scales[:, c, a * P : (a + 1) * P],
-                        rhs=h_codes[:, c, :].bitcast(FP8X4),
-                        rhs_scale=h_scales[:, c, :],
-                        start=(c == 0),
-                        stop=(c == PASSES2 - 1),
-                    )
-                nc.scalar.activation(
-                    out=m_relu[:, a, :],
-                    in_=m_ps[:],
-                    func=ACT.Relu,
-                    bias=bias_cols[:, F_TILES + a : F_TILES + a + 1],
-                    scale=1.0,
-                )
-
-            stats = work.tile([P, TILES, 6], F32)
-            mean_var = work.tile([P, TILES, 2], F32)
-            centred_gain = work.tile([P, TILES, E], F32)
-            for j in range(TILES):
-                y_ps = psum.tile([P, E], F32, tag="y_ps")
-                nc.tensor.matmul(
-                    out=y_ps[:], lhsT=ident_bf16[:], rhs=x_sb[g][:, j, :], start=True, stop=False
-                )
-                for a in range(E_TILES):
-                    nc.tensor.matmul(
-                        out=y_ps[:, a * P : (a + 1) * P],
-                        lhsT=m_relu[:, a, j * P : (j + 1) * P],
-                        rhs=ident_f32[:],
-                        is_transpose=True,
-                        start=False,
-                        stop=(a == E_TILES - 1),
-                    )
-                nc.vector.bn_stats(out=stats[:, j, :], in_=y_ps[:])
-                nc.vector.bn_aggr(out=mean_var[:, j, :], in_=stats[:, j, :])
-                nc.vector.scalar_tensor_tensor(
-                    out=centred_gain[:, j, :],
-                    in0=y_ps[:],
-                    scalar=mean_var[:, j, 0:1],
-                    in1=gain[:],
-                    op0=ALU.subtract,
-                    op1=ALU.mult,
-                )
-            std = work.tile([P, TILES], F32)
-            nc.scalar.activation(
-                out=std[:], in_=mean_var[:, :, 1], func=ACT.Sqrt, bias=eps[:], scale=1.0
-            )
-            rstd = work.tile([P, TILES], F32)
-            nc.vector.reciprocal(out=rstd[:], in_=std[:])
-            result = work.tile([P, TILES, E], F32)
-            for j in range(TILES):
-                nc.vector.scalar_tensor_tensor(
-                    out=result[:, j, :],
-                    in0=centred_gain[:, j, :],
-                    scalar=rstd[:, j : j + 1],
-                    in1=shift[:],
-                    op0=ALU.mult,
-                    op1=ALU.add,
-                )
-                nc.sync.dma_start(out=out_rows[g][:, j, :], in_=result[:, j, :])
+                second_matmul(f, a)
+            scale_shift_store(f - 1)
+            for c in range(PASSES2):
+                quantise_h(f + 1, c)
+            for c in range(PASSES2):
+                for t in range(PACK):
+                    first_matmul(f + 2, c * PACK + t)
+                interleave_h(f + 2, c)
+                assemble_y(f, 2 * c)
+                assemble_y(f, 2 * c + 1)
+                transpose_x(f + 4, c)
+                centre_and_gain(f, 2 * c)
+                centre_and_gain(f, 2 * c + 1)
+            standard_deviation(f)
+            quantise_x(f + 4)

@@ -238,23 +238,31 @@ def tile_transformerdecoderblock_pb_t_kernel(
                     stop=(a == E_TILES - 1),
                 )
 
-        def centre_and_gain(g, j):
+        def statistics(g, tiles):
             if not exists(g):
                 return
-            if j == 0:
+            if tiles[0] == 0:
                 stats[g] = work.tile([P, TILES, 6], F32, name="stats")
                 mean_var[g] = work.tile([P, TILES, 2], F32, name="mean_var")
+            for j in tiles:
+                nc.vector.bn_stats(out=stats[g][:, j, :], in_=y_ps[g, j][:])
+            for j in tiles:
+                nc.vector.bn_aggr(out=mean_var[g][:, j, :], in_=stats[g][:, j, :])
+
+        def centre_and_gain(g, tiles):
+            if not exists(g):
+                return
+            if tiles[0] == 0:
                 centred_gain[g] = work.tile([P, TILES, E], F32, name="centred_gain")
-            nc.vector.bn_stats(out=stats[g][:, j, :], in_=y_ps[g, j][:])
-            nc.vector.bn_aggr(out=mean_var[g][:, j, :], in_=stats[g][:, j, :])
-            nc.vector.scalar_tensor_tensor(
-                out=centred_gain[g][:, j, :],
-                in0=y_ps[g, j][:],
-                scalar=mean_var[g][:, j, 0:1],
-                in1=gain[:],
-                op0=ALU.subtract,
-                op1=ALU.mult,
-            )
+            for j in tiles:
+                nc.vector.scalar_tensor_tensor(
+                    out=centred_gain[g][:, j, :],
+                    in0=y_ps[g, j][:],
+                    scalar=mean_var[g][:, j, 0:1],
+                    in1=gain[:],
+                    op0=ALU.subtract,
+                    op1=ALU.mult,
+                )
 
         def standard_deviation(g):
             if not exists(g):
@@ -264,11 +272,15 @@ def tile_transformerdecoderblock_pb_t_kernel(
                 out=std[g][:], in_=mean_var[g][:, :, 1], func=ACT.Sqrt, bias=eps[:], scale=1.0
             )
 
-        def scale_shift_store(g):
+        def inverse_std(g):
             if not exists(g):
                 return
             rstd[g] = work.tile([P, TILES], F32, name="rstd")
             nc.vector.reciprocal(out=rstd[g][:], in_=std[g][:])
+
+        def scale_shift_store(g):
+            if not exists(g):
+                return
             for j in range(TILES):
                 result = work.tile([P, E], F32, bufs=4)
                 nc.vector.scalar_tensor_tensor(
@@ -295,7 +307,6 @@ def tile_transformerdecoderblock_pb_t_kernel(
         quantise(nc, w1_codes[:, halves[0]], w1_scales[:, halves[0]], w1_grouped[:, halves[0], :])
         interleave(nc, w1_grouped[:, halves[1], :], w1_raw[:, :, halves[1]])
         quantise(nc, w1_codes[:, halves[1]], w1_scales[:, halves[1]], w1_grouped[:, halves[1], :])
-        quantise_x(1)
         for c in range(PASSES2):
             interleave(nc, w2_grouped[:, c, :, :], w2_raw[:, c * PACK : (c + 1) * PACK, :])
         for c in range(PASSES2):
@@ -304,17 +315,20 @@ def tile_transformerdecoderblock_pb_t_kernel(
         for f in range(-2, N_GROUPS + 1):
             for a in range(E_TILES):
                 second_matmul(f, a)
-            scale_shift_store(f - 1)
+            inverse_std(f - 1)
             for c in range(PASSES2):
                 quantise_h(f + 1, c)
+            scale_shift_store(f - 1)
             for c in range(PASSES2):
+                pair = (2 * c, 2 * c + 1)
                 for t in range(PACK):
                     first_matmul(f + 2, c * PACK + t)
                 interleave_h(f + 2, c)
-                assemble_y(f, 2 * c)
-                assemble_y(f, 2 * c + 1)
+                for j in pair:
+                    assemble_y(f, j)
                 transpose_x(f + 4, c)
-                centre_and_gain(f, 2 * c)
-                centre_and_gain(f, 2 * c + 1)
+                statistics(f, pair)
+                if c == 1:
+                    quantise_x(f + 3)
+                centre_and_gain(f, pair)
             standard_deviation(f)
-            quantise_x(f + 4)

@@ -37,8 +37,8 @@ def interleave(nc, grouped, planes):
 
 
 def interleave_beside_vector(nc, grouped, planes):
-    for j in range(TILES):
-        cols = slice(j * P, (j + 1) * P)
+    for piece in range(2):
+        cols = slice(piece * GROUP // 2, (piece + 1) * GROUP // 2)
         nc.gpsimd.tensor_scalar(
             out=grouped[:, cols, :],
             in0=planes[:, :, cols].rearrange("p t c -> p c t"),
@@ -316,9 +316,10 @@ def tile_transformerdecoderblock_pb_t_kernel(
             for a in range(E_TILES):
                 second_matmul(f, a)
             inverse_std(f - 1)
+            scale_shift_store(f - 1)
             for c in range(PASSES2):
                 quantise_h(f + 1, c)
-            scale_shift_store(f - 1)
+            quantise_x(f + 3)
             for c in range(PASSES2):
                 pair = (2 * c, 2 * c + 1)
                 for t in range(PACK):
@@ -328,7 +329,5 @@ def tile_transformerdecoderblock_pb_t_kernel(
                     assemble_y(f, j)
                 transpose_x(f + 4, c)
                 statistics(f, pair)
-                if c == 1:
-                    quantise_x(f + 3)
                 centre_and_gain(f, pair)
             standard_deviation(f)

@@ -108,7 +108,7 @@ def tile_transformerdecoderblock_pb_t_kernel(
         eps = keep.tile([P, 1], F32)
         nc.vector.memset(eps[:], EPS)
         table_warm = keep.tile([P, 1], F32)
-        nc.scalar.activation(out=table_warm[:], in_=eps[:], func=ACT.Sqrt)
+        nc.scalar.activation(out=table_warm[:], in_=eps[:], func=ACT.Abs_reciprocal_sqrt)
 
         w1_grouped = keep.tile([P, F, PACK], BF16, align_bytes=64)
         w1_codes = keep.tile([P, F], U32, align_bytes=64)
@@ -121,7 +121,7 @@ def tile_transformerdecoderblock_pb_t_kernel(
 
         x_grouped, x_codes, x_scales = {}, {}, {}
         h_planes, h_grouped, h_codes, h_scales = {}, {}, {}, {}
-        m_relu, y_ps, stats, mean_var, centred_gain, std, rstd = {}, {}, {}, {}, {}, {}, {}
+        m_relu, y_ps, stats, mean_var, centred_gain, rstd = {}, {}, {}, {}, {}, {}
 
         def exists(g):
             return 0 <= g < N_GROUPS
@@ -264,19 +264,17 @@ def tile_transformerdecoderblock_pb_t_kernel(
                     op1=ALU.mult,
                 )
 
-        def standard_deviation(g):
-            if not exists(g):
-                return
-            std[g] = work.tile([P, TILES], F32, name="std")
-            nc.scalar.activation(
-                out=std[g][:], in_=mean_var[g][:, :, 1], func=ACT.Sqrt, bias=eps[:], scale=1.0
-            )
-
         def inverse_std(g):
             if not exists(g):
                 return
             rstd[g] = work.tile([P, TILES], F32, name="rstd")
-            nc.vector.reciprocal(out=rstd[g][:], in_=std[g][:])
+            nc.scalar.activation(
+                out=rstd[g][:],
+                in_=mean_var[g][:, :, 1],
+                func=ACT.Abs_reciprocal_sqrt,
+                bias=eps[:],
+                scale=1.0,
+            )
 
         def scale_shift_store(g):
             if not exists(g):
@@ -315,7 +313,6 @@ def tile_transformerdecoderblock_pb_t_kernel(
         for f in range(-2, N_GROUPS + 1):
             for a in range(E_TILES):
                 second_matmul(f, a)
-            inverse_std(f - 1)
             scale_shift_store(f - 1)
             for c in range(PASSES2):
                 quantise_h(f + 1, c)
@@ -327,7 +324,9 @@ def tile_transformerdecoderblock_pb_t_kernel(
                 interleave_h(f + 2, c)
                 for j in pair:
                     assemble_y(f, j)
-                transpose_x(f + 4, c)
+                if c == 1:
+                    transpose_x(f + 4, 0)
+                    transpose_x(f + 4, 1)
                 statistics(f, pair)
                 centre_and_gain(f, pair)
-            standard_deviation(f)
+            inverse_std(f)

@@ -238,16 +238,17 @@ def tile_transformerdecoderblock_pb_t_kernel(
                     stop=(a == E_TILES - 1),
                 )
 
-        def statistics(g, tiles):
-            if not exists(g):
-                return
-            if tiles[0] == 0:
-                stats[g] = work.tile([P, TILES, 6], F32, name="stats")
-                mean_var[g] = work.tile([P, TILES, 2], F32, name="mean_var")
-            for j in tiles:
-                nc.vector.bn_stats(out=stats[g][:, j, :], in_=y_ps[g, j][:])
-            for j in tiles:
-                nc.vector.bn_aggr(out=mean_var[g][:, j, :], in_=stats[g][:, j, :])
+        def statistics(g, tiles, last_pass_tile):
+            if exists(g):
+                if tiles[0] == 0:
+                    stats[g] = work.tile([P, TILES, 6], F32, name="stats")
+                    mean_var[g] = work.tile([P, TILES, 2], F32, name="mean_var")
+                for j in tiles:
+                    nc.vector.bn_stats(out=stats[g][:, j, :], in_=y_ps[g, j][:])
+                nc.vector.bn_aggr(out=mean_var[g][:, tiles[0], :], in_=stats[g][:, tiles[0], :])
+            scale_shift_store(g - 1, last_pass_tile)
+            if exists(g):
+                nc.vector.bn_aggr(out=mean_var[g][:, tiles[1], :], in_=stats[g][:, tiles[1], :])
 
         def centre_and_gain(g, tiles):
             if not exists(g):
@@ -276,20 +277,19 @@ def tile_transformerdecoderblock_pb_t_kernel(
                 scale=1.0,
             )
 
-        def scale_shift_store(g):
+        def scale_shift_store(g, j):
             if not exists(g):
                 return
-            for j in range(TILES):
-                result = work.tile([P, E], F32, bufs=4)
-                nc.vector.scalar_tensor_tensor(
-                    out=result[:],
-                    in0=centred_gain[g][:, j, :],
-                    scalar=rstd[g][:, j : j + 1],
-                    in1=shift_ps[:],
-                    op0=ALU.mult,
-                    op1=ALU.add,
-                )
-                nc.sync.dma_start(out=out_rows[g][:, j, :], in_=result[:])
+            result = work.tile([P, E], F32, bufs=4)
+            nc.vector.scalar_tensor_tensor(
+                out=result[:],
+                in0=centred_gain[g][:, j, :],
+                scalar=rstd[g][:, j : j + 1],
+                in1=shift_ps[:],
+                op0=ALU.mult,
+                op1=ALU.add,
+            )
+            nc.sync.dma_start(out=out_rows[g][:, j, :], in_=result[:])
 
         transpose_x(0, 0)
         transpose_x(0, 1)
@@ -313,7 +313,8 @@ def tile_transformerdecoderblock_pb_t_kernel(
         for f in range(-2, N_GROUPS + 1):
             for a in range(E_TILES):
                 second_matmul(f, a)
-            scale_shift_store(f - 1)
+            scale_shift_store(f - 1, 0)
+            scale_shift_store(f - 1, 1)
             for c in range(PASSES2):
                 quantise_h(f + 1, c)
             quantise_x(f + 3)
@@ -327,6 +328,6 @@ def tile_transformerdecoderblock_pb_t_kernel(
                 if c == 1:
                     transpose_x(f + 4, 0)
                     transpose_x(f + 4, 1)
-                statistics(f, pair)
+                statistics(f, pair, 2 + c)
                 centre_and_gain(f, pair)
             inverse_std(f)

@@ -221,22 +221,24 @@ def tile_transformerdecoderblock_pb_t_kernel(
                 scale=1.0,
             )
 
-        def assemble_y(g, j):
+        def assemble_y(g, tiles):
             if not exists(g):
                 return
-            y_ps[g, j] = psum.tile([P, E], F32, name="y_ps", tag="bank")
-            nc.tensor.matmul(
-                out=y_ps[g, j][:], lhsT=ident_bf16[:], rhs=x_sb[g][:, j, :], start=True, stop=False
-            )
-            for a in range(E_TILES):
+            for j in tiles:
+                y_ps[g, j] = psum.tile([P, E], F32, name="y_ps", tag="bank")
                 nc.tensor.matmul(
-                    out=y_ps[g, j][:, a * P : (a + 1) * P],
-                    lhsT=m_relu[g][:, a, j * P : (j + 1) * P],
-                    rhs=ident_f32[:],
-                    is_transpose=True,
-                    start=False,
-                    stop=(a == E_TILES - 1),
+                    out=y_ps[g, j][:], lhsT=ident_bf16[:], rhs=x_sb[g][:, j, :], start=True, stop=False
                 )
+            for j in tiles:
+                for a in range(E_TILES):
+                    nc.tensor.matmul(
+                        out=y_ps[g, j][:, a * P : (a + 1) * P],
+                        lhsT=m_relu[g][:, a, j * P : (j + 1) * P],
+                        rhs=ident_f32[:],
+                        is_transpose=True,
+                        start=False,
+                        stop=(a == E_TILES - 1),
+                    )
 
         def statistics(g, tiles, last_pass_tile):
             if exists(g):
@@ -323,8 +325,7 @@ def tile_transformerdecoderblock_pb_t_kernel(
                 for t in range(PACK):
                     first_matmul(f + 2, c * PACK + t)
                 interleave_h(f + 2, c)
-                for j in pair:
-                    assemble_y(f, j)
+                assemble_y(f, pair)
                 if c == 1:
                     transpose_x(f + 4, 0)
                     transpose_x(f + 4, 1)

@@ -245,12 +245,35 @@ def tile_transformerdecoderblock_pb_t_kernel(
                 if tiles[0] == 0:
                     stats[g] = work.tile([P, TILES, 6], F32, name="stats")
                     mean_var[g] = work.tile([P, TILES, 2], F32, name="mean_var")
-                for j in tiles:
-                    nc.vector.bn_stats(out=stats[g][:, j, :], in_=y_ps[g, j][:])
+                nc.vector.bn_stats(out=stats[g][:, tiles[0], :], in_=y_ps[g, tiles[0]][:])
+                if scalar_is_free(g):
+                    statistics_on_scalar(g, tiles[1])
+                else:
+                    nc.vector.bn_stats(out=stats[g][:, tiles[1], :], in_=y_ps[g, tiles[1]][:])
                 nc.vector.bn_aggr(out=mean_var[g][:, tiles[0], :], in_=stats[g][:, tiles[0], :])
             scale_shift_store(g - 1, last_pass_tile)
-            if exists(g):
+            if exists(g) and not scalar_is_free(g):
                 nc.vector.bn_aggr(out=mean_var[g][:, tiles[1], :], in_=stats[g][:, tiles[1], :])
+
+        def scalar_is_free(g):
+            return g + 2 >= N_GROUPS
+
+        def statistics_on_scalar(g, j):
+            total = stats[g][:, j, 0:1]
+            squares = stats[g][:, j, 1:2]
+            unused = work.tile([P, E], BF16, name="unused")
+            nc.scalar.activation(out=unused[:], in_=y_ps[g, j][:], func=ACT.Identity, accum_out=total)
+            nc.scalar.activation(out=mean_var[g][:, j, 0:1], in_=total, func=ACT.Copy, scale=1.0 / E)
+            unused = work.tile([P, E], BF16, name="unused")
+            nc.scalar.activation(
+                out=unused[:],
+                in_=y_ps[g, j][:],
+                func=ACT.Square,
+                bias=mean_var[g][:, j, 0:1],
+                scale=-1.0,
+                accum_out=squares,
+            )
+            nc.scalar.activation(out=mean_var[g][:, j, 1:2], in_=squares, func=ACT.Copy, scale=1.0 / E)
 
         def centre_and_gain(g, tiles):
             if not exists(g):

@@ -187,7 +187,10 @@ def tile_transformerdecoderblock_pb_t_kernel(
                 h_grouped[g] = work.tile(
                     [P, PASSES2, GROUP, PACK], BF16, name="h_grouped", align_bytes=64
                 )
-            interleave_beside_vector(nc, h_grouped[g][:, c, :, :], h_planes[g, c][:])
+            if g < 2:
+                interleave(nc, h_grouped[g][:, c, :, :], h_planes[g, c][:])
+            else:
+                interleave_beside_vector(nc, h_grouped[g][:, c, :, :], h_planes[g, c][:])
 
         def quantise_h(g, c):
             if not exists(g):

@@ -333,6 +333,7 @@ def tile_transformerdecoderblock_pb_t_kernel(
         quantise(nc, w1_codes[:, halves[0]], w1_scales[:, halves[0]], w1_grouped[:, halves[0], :])
         interleave(nc, w1_grouped[:, halves[1], :], w1_raw[:, :, halves[1]])
         quantise(nc, w1_codes[:, halves[1]], w1_scales[:, halves[1]], w1_grouped[:, halves[1], :])
+        quantise_x(1)
         for c in range(PASSES2):
             interleave(nc, w2_grouped[:, c, :, :], w2_raw[:, c * PACK : (c + 1) * PACK, :])
         for c in range(PASSES2):
@@ -345,14 +346,21 @@ def tile_transformerdecoderblock_pb_t_kernel(
             scale_shift_store(f - 1, 1)
             for c in range(PASSES2):
                 quantise_h(f + 1, c)
-            quantise_x(f + 3)
+            if f + 3 > 1:
+                quantise_x(f + 3)
             for c in range(PASSES2):
                 pair = (2 * c, 2 * c + 1)
-                for t in range(PACK):
-                    first_matmul(f + 2, c * PACK + t)
-                interleave_h(f + 2, c)
-                assemble_y(f, pair)
-                if c == 1:
+                if c == 0:
+                    for t in range(PACK):
+                        first_matmul(f + 2, t)
+                    interleave_h(f + 2, c)
+                    assemble_y(f, pair)
+                else:
+                    for t in range(PACK - 1):
+                        first_matmul(f + 2, PACK + t)
+                    assemble_y(f, pair)
+                    first_matmul(f + 2, 2 * PACK - 1)
+                    interleave_h(f + 2, c)
                     transpose_x(f + 4, 0)
                     transpose_x(f + 4, 1)
                 statistics(f, pair, 2 + c)

@@ -95,9 +95,10 @@ def tile_transformerdecoderblock_pb_t_kernel(
                 )
         nc.sync.dma_start(out=x_sb[1][:], in_=x_rows[1])
         nc.sync.dma_start(out=w2_raw[:], in_=mlp_w2.rearrange("(a p) e -> p a e", p=P))
-        nc.sync.dma_start(out=gain[:], in_=ln3_g.partition_broadcast(P))
         for g in range(2, N_GROUPS):
             nc.sync.dma_start(out=x_sb[g][:], in_=x_rows[g])
+            if g == 3:
+                nc.sync.dma_start(out=gain[:], in_=ln3_g.partition_broadcast(P))
 
         ident_f32 = keep.tile([P, P], F32)
         make_identity(nc, ident_f32[:])

@@ -249,25 +249,29 @@ def tile_transformerdecoderblock_pb_t_kernel(
                 if tiles[0] == 0:
                     stats[g] = work.tile([P, TILES, 6], F32, name="stats")
                     mean_var[g] = work.tile([P, TILES, 2], F32, name="mean_var")
-                nc.vector.bn_stats(out=stats[g][:, tiles[0], :], in_=y_ps[g, tiles[0]][:])
-                if scalar_is_free(g):
-                    statistics_on_scalar(g, tiles[1])
-                else:
-                    nc.vector.bn_stats(out=stats[g][:, tiles[1], :], in_=y_ps[g, tiles[1]][:])
-                nc.vector.bn_aggr(out=mean_var[g][:, tiles[0], :], in_=stats[g][:, tiles[0], :])
-            scale_shift_store(g - 1, last_pass_tile)
-            if exists(g) and not scalar_is_free(g):
-                nc.vector.bn_aggr(out=mean_var[g][:, tiles[1], :], in_=stats[g][:, tiles[1], :])
+                for j in tiles:
+                    if on_scalar(g, j):
+                        statistics_on_scalar(g, j)
+                    else:
+                        nc.vector.bn_stats(out=stats[g][:, j, :], in_=y_ps[g, j][:])
+            for j in tiles:
+                if exists(g) and not on_scalar(g, j):
+                    nc.vector.bn_aggr(out=mean_var[g][:, j, :], in_=stats[g][:, j, :])
+                if j == tiles[0]:
+                    scale_shift_store(g - 1, last_pass_tile)
 
-        def scalar_is_free(g):
-            return g + 2 >= N_GROUPS
+        def on_scalar(g, j):
+            return g + 2 >= N_GROUPS and (j % 2 == 1 or (g, j) == (N_GROUPS - 1, 2))
 
         def statistics_on_scalar(g, j):
-            total = stats[g][:, j, 0:1]
-            squares = stats[g][:, j, 1:2]
             unused = work.tile([P, E], BF16, name="unused")
-            nc.scalar.activation(out=unused[:], in_=y_ps[g, j][:], func=ACT.Identity, accum_out=total)
-            nc.scalar.activation(out=mean_var[g][:, j, 0:1], in_=total, func=ACT.Copy, scale=1.0 / E)
+            nc.scalar.activation(
+                out=unused[:],
+                in_=y_ps[g, j][:],
+                func=ACT.Identity,
+                scale=1.0 / E,
+                accum_out=mean_var[g][:, j, 0:1],
+            )
             unused = work.tile([P, E], BF16, name="unused")
             nc.scalar.activation(
                 out=unused[:],
@@ -275,9 +279,8 @@ def tile_transformerdecoderblock_pb_t_kernel(
                 func=ACT.Square,
                 bias=mean_var[g][:, j, 0:1],
                 scale=-1.0,
-                accum_out=squares,
+                accum_out=mean_var[g][:, j, 1:2],
             )
-            nc.scalar.activation(out=mean_var[g][:, j, 1:2], in_=squares, func=ACT.Copy, scale=1.0 / E)
 
         def centre_and_gain(g, tiles):
             if not exists(g):
@@ -294,17 +297,22 @@ def tile_transformerdecoderblock_pb_t_kernel(
                     op1=ALU.mult,
                 )
 
-        def inverse_std(g):
+        def inverse_std(g, tiles):
             if not exists(g):
                 return
-            rstd[g] = work.tile([P, TILES], F32, name="rstd")
-            nc.scalar.activation(
-                out=rstd[g][:],
-                in_=mean_var[g][:, :, 1],
-                func=ACT.Abs_reciprocal_sqrt,
-                bias=eps[:],
-                scale=1.0,
-            )
+            if tiles[0] == 0:
+                rstd[g] = work.tile([P, TILES], F32, name="rstd")
+            for kind in (False, True):
+                of_kind = [j for j in tiles if on_scalar(g, j) == kind]
+                if of_kind:
+                    part = slice(of_kind[0], of_kind[-1] + 1, of_kind[1] - of_kind[0] if len(of_kind) > 1 else 1)
+                    nc.scalar.activation(
+                        out=rstd[g][:, part],
+                        in_=mean_var[g][:, part, 1],
+                        func=ACT.Abs_reciprocal_sqrt,
+                        bias=eps[:],
+                        scale=1.0 / E if kind else 1.0,
+                    )
 
         def scale_shift_store(g, j):
             if not exists(g):
@@ -340,7 +348,7 @@ def tile_transformerdecoderblock_pb_t_kernel(
         for c in range(PASSES2):
             quantise(nc, w2_codes[:, c, :], w2_scales[:, c, :], w2_grouped[:, c, :, :])
 
-        for f in range(-2, N_GROUPS + 1):
+        for f in range(-2, N_GROUPS):
             for a in range(E_TILES):
                 second_matmul(f, a)
             scale_shift_store(f - 1, 0)
@@ -366,4 +374,9 @@ def tile_transformerdecoderblock_pb_t_kernel(
                     transpose_x(f + 4, 1)
                 statistics(f, pair, 2 + c)
                 centre_and_gain(f, pair)
-            inverse_std(f)
+                if f == N_GROUPS - 1:
+                    inverse_std(f, pair)
+                    for j in pair:
+                        scale_shift_store(f, j)
+            if f < N_GROUPS - 1:
+                inverse_std(f, range(TILES))

@@ -351,6 +351,8 @@ def tile_transformerdecoderblock_pb_t_kernel(
         for f in range(-2, N_GROUPS):
             for a in range(E_TILES):
                 second_matmul(f, a)
+                if a == 0 and exists(f) and f > 0:
+                    inverse_std(f - 1, range(TILES))
             scale_shift_store(f - 1, 0)
             scale_shift_store(f - 1, 1)
             for c in range(PASSES2):
@@ -378,5 +380,3 @@ def tile_transformerdecoderblock_pb_t_kernel(
                     inverse_std(f, pair)
                     for j in pair:
                         scale_shift_store(f, j)
-            if f < N_GROUPS - 1:
-                inverse_std(f, range(TILES))

@@ -244,21 +244,20 @@ def tile_transformerdecoderblock_pb_t_kernel(
                         stop=(a == E_TILES - 1),
                     )
 
-        def statistics(g, tiles, last_pass_tile):
-            if exists(g):
-                if tiles[0] == 0:
-                    stats[g] = work.tile([P, TILES, 6], F32, name="stats")
-                    mean_var[g] = work.tile([P, TILES, 2], F32, name="mean_var")
-                for j in tiles:
-                    if on_scalar(g, j):
-                        statistics_on_scalar(g, j)
-                    else:
-                        nc.vector.bn_stats(out=stats[g][:, j, :], in_=y_ps[g, j][:])
-            for j in tiles:
-                if exists(g) and not on_scalar(g, j):
-                    nc.vector.bn_aggr(out=mean_var[g][:, j, :], in_=stats[g][:, j, :])
-                if j == tiles[0]:
-                    scale_shift_store(g - 1, last_pass_tile)
+        def tile_statistics(g, j):
+            if not exists(g):
+                return
+            if j == 0:
+                stats[g] = work.tile([P, TILES, 6], F32, name="stats")
+                mean_var[g] = work.tile([P, TILES, 2], F32, name="mean_var")
+            if on_scalar(g, j):
+                statistics_on_scalar(g, j)
+            else:
+                nc.vector.bn_stats(out=stats[g][:, j, :], in_=y_ps[g, j][:])
+
+        def aggregate(g, j):
+            if exists(g) and not on_scalar(g, j):
+                nc.vector.bn_aggr(out=mean_var[g][:, j, :], in_=stats[g][:, j, :])
 
         def on_scalar(g, j):
             return g + 2 >= N_GROUPS and (j % 2 == 1 or (g, j) == (N_GROUPS - 1, 2))
@@ -282,25 +281,24 @@ def tile_transformerdecoderblock_pb_t_kernel(
                 accum_out=mean_var[g][:, j, 1:2],
             )
 
-        def centre_and_gain(g, tiles):
+        def centre_and_gain(g, j):
             if not exists(g):
                 return
-            if tiles[0] == 0:
+            if g not in centred_gain:
                 centred_gain[g] = work.tile([P, TILES, E], F32, name="centred_gain")
-            for j in tiles:
-                nc.vector.scalar_tensor_tensor(
-                    out=centred_gain[g][:, j, :],
-                    in0=y_ps[g, j][:],
-                    scalar=mean_var[g][:, j, 0:1],
-                    in1=gain[:],
-                    op0=ALU.subtract,
-                    op1=ALU.mult,
-                )
+            nc.vector.scalar_tensor_tensor(
+                out=centred_gain[g][:, j, :],
+                in0=y_ps[g, j][:],
+                scalar=mean_var[g][:, j, 0:1],
+                in1=gain[:],
+                op0=ALU.subtract,
+                op1=ALU.mult,
+            )
 
         def inverse_std(g, tiles):
             if not exists(g):
                 return
-            if tiles[0] == 0:
+            if g not in rstd:
                 rstd[g] = work.tile([P, TILES], F32, name="rstd")
             for kind in (False, True):
                 of_kind = [j for j in tiles if on_scalar(g, j) == kind]
@@ -348,7 +346,7 @@ def tile_transformerdecoderblock_pb_t_kernel(
         for c in range(PASSES2):
             quantise(nc, w2_codes[:, c, :], w2_scales[:, c, :], w2_grouped[:, c, :, :])
 
-        for f in range(-2, N_GROUPS):
+        for f in range(-2, N_GROUPS - 2):
             for a in range(E_TILES):
                 second_matmul(f, a)
                 if a == 0 and exists(f) and f > 0:
@@ -374,9 +372,61 @@ def tile_transformerdecoderblock_pb_t_kernel(
                     interleave_h(f + 2, c)
                     transpose_x(f + 4, 0)
                     transpose_x(f + 4, 1)
-                statistics(f, pair, 2 + c)
-                centre_and_gain(f, pair)
-                if f == N_GROUPS - 1:
-                    inverse_std(f, pair)
-                    for j in pair:
-                        scale_shift_store(f, j)
+                tile_statistics(f, pair[0])
+                tile_statistics(f, pair[1])
+                aggregate(f, pair[0])
+                scale_shift_store(f - 1, 2 + c)
+                aggregate(f, pair[1])
+                centre_and_gain(f, pair[0])
+                centre_and_gain(f, pair[1])
+
+        p, q = N_GROUPS - 2, N_GROUPS - 1
+        second_matmul(p, 0)
+        second_matmul(p, 1)
+        inverse_std(p - 1, range(TILES))
+        second_matmul(p, 2)
+        second_matmul(p, 3)
+        scale_shift_store(p - 1, 0)
+        scale_shift_store(p - 1, 1)
+        assemble_y(p, (0, 1))
+        tile_statistics(p, 0)
+        quantise_h(q, 0)
+        quantise_h(q, 1)
+        assemble_y(p, (2, 3))
+        tile_statistics(p, 1)
+        tile_statistics(p, 3)
+        aggregate(p, 0)
+        for a in range(3):
+            second_matmul(q, a)
+        tile_statistics(p, 2)
+        scale_shift_store(p - 1, 2)
+        centre_and_gain(p, 0)
+        centre_and_gain(p, 1)
+        aggregate(p, 2)
+        scale_shift_store(p - 1, 3)
+        centre_and_gain(p, 2)
+        centre_and_gain(p, 3)
+        inverse_std(p, range(TILES))
+        second_matmul(q, 3)
+        scale_shift_store(p, 0)
+        scale_shift_store(p, 1)
+        assemble_y(q, (0, 1))
+        tile_statistics(q, 0)
+        tile_statistics(q, 1)
+        scale_shift_store(p, 2)
+        aggregate(q, 0)
+        assemble_y(q, (2, 3))
+        tile_statistics(q, 2)
+        inverse_std(q, (0, 1))
+        tile_statistics(q, 3)
+        scale_shift_store(p, 3)
+        centre_and_gain(q, 0)
+        centre_and_gain(q, 1)
+        scale_shift_store(q, 0)
+        scale_shift_store(q, 1)
+        centre_and_gain(q, 2)
+        inverse_std(q, (2,))
+        centre_and_gain(q, 3)
+        inverse_std(q, (3,))
+        scale_shift_store(q, 2)
+        scale_shift_store(q, 3)

@@ -24,6 +24,8 @@ TILES = GROUP // P
 F_TILES = F // P
 E_TILES = E // P
 PASSES2 = F // K_PASS
+BANKS = 7
+HELD = 4
 RUN = 4
 
 FLOPS = 2 * TOKENS * E * F * 2
@@ -68,7 +70,7 @@ def tile_transformerdecoderblock_pb_t_kernel(
         stack.enter_context(tc.manual_schedule())
         keep = stack.enter_context(tc.tile_pool(name="keep", bufs=1))
         work = stack.enter_context(tc.tile_pool(name="work", bufs=2))
-        psum = stack.enter_context(tc.psum_pool(name="psum", bufs=7))
+        psum = stack.enter_context(tc.psum_pool(name="psum", bufs=1))
 
         x_sb = [keep.tile([P, TILES, E], BF16, name="x%d" % g) for g in range(N_GROUPS)]
         w1_raw = keep.tile([P, PACK, F], BF16)
@@ -118,11 +120,26 @@ def tile_transformerdecoderblock_pb_t_kernel(
         w2_codes = keep.tile([P, PASSES2, E], U32, align_bytes=64)
         w2_scales = keep.tile([P, PASSES2, E], U8, align_bytes=64)
         bias_cols = keep.tile([P, F_TILES + E_TILES], F32)
-        shift_ps = psum.tile([P, E], F32, tag="shift_ps", bufs=1)
+        shift_ps = psum.tile([P, E], F32, tag="shift_ps")
 
         x_grouped, x_codes, x_scales = {}, {}, {}
         h_planes, h_grouped, h_codes, h_scales = {}, {}, {}, {}
         m_relu, y_ps, stats, mean_var, centred_gain, rstd = {}, {}, {}, {}, {}, {}
+
+        free_banks = list(range(BANKS))
+        held_banks = []
+
+        def next_bank(hold):
+            for entry in held_banks:
+                entry[0] -= 1
+            while held_banks and held_banks[0][0] == 0:
+                free_banks.append(held_banks.pop(0)[1])
+            bank = free_banks.pop(0)
+            if hold:
+                held_banks.append([hold, bank])
+            else:
+                free_banks.append(bank)
+            return "bank%d" % bank
 
         def exists(g):
             return 0 <= g < N_GROUPS
@@ -138,7 +155,7 @@ def tile_transformerdecoderblock_pb_t_kernel(
                 .bitcast(F32)
                 .rearrange("p (c u) -> p c u", u=2)
             )
-            xt = psum.tile([P, 2, 2 * P], F32, tag="bank")
+            xt = psum.tile([P, 2, 2 * P], F32, tag=next_bank(0))
             for jj in range(2):
                 words = x_sb[g][:, 2 * half + jj, :].bitcast(F32)
                 for u in range(2):
@@ -163,7 +180,7 @@ def tile_transformerdecoderblock_pb_t_kernel(
             c, t = divmod(a, PACK)
             if t == 0:
                 h_planes[g, c] = work.tile([P, PACK, GROUP], BF16, name="h_planes", bufs=4)
-            h_ps = psum.tile([P, GROUP], F32, tag="bank")
+            h_ps = psum.tile([P, GROUP], F32, tag=next_bank(0))
             nc.tensor.matmul_mx(
                 out=h_ps[:],
                 lhsT=w1_codes[:, a * P : (a + 1) * P].bitcast(FP8X4),
@@ -206,7 +223,7 @@ def tile_transformerdecoderblock_pb_t_kernel(
                 return
             if a == 0:
                 m_relu[g] = work.tile([P, E_TILES, GROUP], F32, name="m_relu")
-            m_ps = psum.tile([P, GROUP], F32, tag="bank")
+            m_ps = psum.tile([P, GROUP], F32, tag=next_bank(0))
             for c in range(PASSES2):
                 nc.tensor.matmul_mx(
                     out=m_ps[:],
@@ -229,7 +246,7 @@ def tile_transformerdecoderblock_pb_t_kernel(
             if not exists(g):
                 return
             for j in tiles:
-                y_ps[g, j] = psum.tile([P, E], F32, name="y_ps", tag="bank")
+                y_ps[g, j] = psum.tile([P, E], F32, name="y_ps", tag=next_bank(HELD))
                 nc.tensor.matmul(
                     out=y_ps[g, j][:], lhsT=ident_bf16[:], rhs=x_sb[g][:, j, :], start=True, stop=False
                 )
@@ -328,7 +345,7 @@ def tile_transformerdecoderblock_pb_t_kernel(
 
         transpose_x(0, 0)
         transpose_x(0, 1)
-        bias_ps = psum.tile([P, P], BF16, tag="bank")
+        bias_ps = psum.tile([P, P], BF16, tag=next_bank(0))
         nc.tensor.transpose(bias_ps[:], bias_rows[:], ident_bf16[:])
         nc.vector.tensor_copy(out=bias_cols[:], in_=bias_ps[:, 0 : F_TILES + E_TILES])
         nc.tensor.matmul(out=shift_ps[:], lhsT=ones[:], rhs=shift_row[:], start=True, stop=True)

@@ -190,6 +190,16 @@ def tile_transformerdecoderblock_pb_t_kernel(
                 start=True,
                 stop=True,
             )
+            if (g, a) == (1, 7):
+                nc.vector.tensor_scalar(
+                    out=h_planes[g, c][:, t, :],
+                    in0=h_ps[:],
+                    scalar1=bias_cols[:, a : a + 1],
+                    scalar2=0.0,
+                    op0=ALU.add,
+                    op1=ALU.max,
+                )
+                return
             nc.scalar.activation(
                 out=h_planes[g, c][:, t, :],
                 in_=h_ps[:],
@@ -370,8 +380,9 @@ def tile_transformerdecoderblock_pb_t_kernel(
                     inverse_std(f - 1, range(TILES))
             scale_shift_store(f - 1, 0)
             scale_shift_store(f - 1, 1)
-            for c in range(PASSES2):
-                quantise_h(f + 1, c)
+            quantise_h(f + 1, 0)
+            if f != 0:
+                quantise_h(f + 1, 1)
             if f + 3 > 1:
                 quantise_x(f + 3)
             for c in range(PASSES2):
@@ -392,7 +403,10 @@ def tile_transformerdecoderblock_pb_t_kernel(
                 tile_statistics(f, pair[0])
                 tile_statistics(f, pair[1])
                 aggregate(f, pair[0])
-                scale_shift_store(f - 1, 2 + c)
+                if f == 0 and c == 0:
+                    quantise_h(f + 1, 1)
+                else:
+                    scale_shift_store(f - 1, 2 + c)
                 aggregate(f, pair[1])
                 centre_and_gain(f, pair[0])
                 centre_and_gain(f, pair[1])

@@ -381,9 +381,11 @@ def tile_transformerdecoderblock_pb_t_kernel(
             scale_shift_store(f - 1, 0)
             scale_shift_store(f - 1, 1)
             quantise_h(f + 1, 0)
+            if f >= 1:
+                quantise_x(f + 3)
             if f != 0:
                 quantise_h(f + 1, 1)
-            if f + 3 > 1:
+            if f < 1 and f + 3 > 1:
                 quantise_x(f + 3)
             for c in range(PASSES2):
                 pair = (2 * c, 2 * c + 1)
@@ -393,11 +395,10 @@ def tile_transformerdecoderblock_pb_t_kernel(
                     interleave_h(f + 2, c)
                     assemble_y(f, pair)
                 else:
-                    for t in range(PACK - 1):
+                    for t in range(PACK):
                         first_matmul(f + 2, PACK + t)
-                    assemble_y(f, pair)
-                    first_matmul(f + 2, 2 * PACK - 1)
                     interleave_h(f + 2, c)
+                    assemble_y(f, pair)
                     transpose_x(f + 4, 0)
                     transpose_x(f + 4, 1)
                 tile_statistics(f, pair[0])

from contextlib import ExitStack

import concourse.mybir as mybir
from concourse.masks import make_identity

F32 = mybir.dt.float32
BF16 = mybir.dt.bfloat16
U32 = mybir.dt.uint32
U8 = mybir.dt.uint8
FP8X4 = mybir.dt.float8_e4m3fn_x4
ACT = mybir.ActivationFunctionType
ALU = mybir.AluOpType

P = 128
PACK = 4
K_PASS = P * PACK
TOKENS = 4096
E = 512
F = 1024
EPS = 1e-5
GROUP = 512
N_GROUPS = TOKENS // GROUP
TILES = GROUP // P
F_TILES = F // P
E_TILES = E // P
PASSES2 = F // K_PASS
BANKS = 7
HELD = 4
RUN = 4

FLOPS = 2 * TOKENS * E * F * 2


def interleave(nc, grouped, planes):
    nc.vector.tensor_copy(
        out=grouped.rearrange("p (c i) t -> p c t i", i=RUN),
        in_=planes.rearrange("p t (c i) -> p c t i", i=RUN),
    )


def interleave_beside_vector(nc, grouped, planes):
    for piece in range(2):
        cols = slice(piece * GROUP // 2, (piece + 1) * GROUP // 2)
        nc.gpsimd.tensor_scalar(
            out=grouped[:, cols, :],
            in0=planes[:, :, cols].rearrange("p t c -> p c t"),
            scalar1=1.0,
            scalar2=0.0,
            op0=ALU.mult,
            op1=ALU.add,
        )


def quantise(nc, codes, scales, grouped):
    nc.vector.quantize_mx(
        out=codes.bitcast(FP8X4),
        scales=scales,
        in_=grouped.rearrange("p c t -> p (c t)"),
    )


def tile_transformerdecoderblock_pb_t_kernel(
    tc, x2, mlp_w1, mlp_b1, mlp_w2, mlp_b2, ln3_g, ln3_b, out
):
    nc = tc.nc
    x_rows = x2.flatten_outer_dims().rearrange("(g p j) e -> g p j e", p=P, j=TILES)
    out_rows = out.flatten_outer_dims().rearrange("(g p j) e -> g p j e", p=P, j=TILES)

    with ExitStack() as stack:
        stack.enter_context(tc.manual_schedule())
        keep = stack.enter_context(tc.tile_pool(name="keep", bufs=1))
        work = stack.enter_context(tc.tile_pool(name="work", bufs=2))
        psum = stack.enter_context(tc.psum_pool(name="psum", bufs=1))

        x_sb = [keep.tile([P, TILES, E], BF16, name="x%d" % g) for g in range(N_GROUPS)]
        w1_raw = keep.tile([P, PACK, F], BF16)
        w2_raw = keep.tile([P, PASSES2 * PACK, E], BF16)
        bias_rows = keep.tile([P, P], BF16)
        shift_row = keep.tile([P, E], BF16)
        gain = keep.tile([P, E], BF16)
        halves = [slice(0, F // 2), slice(F // 2, F)]

        nc.vector.memset(bias_rows[:], 0.0)
        nc.vector.memset(shift_row[:], 0.0)
        nc.sync.dma_start(out=x_sb[0][:], in_=x_rows[0])
        nc.sync.dma_start(out=bias_rows[0:F_TILES, :], in_=mlp_b1.rearrange("(a p) -> a p", p=P))
        nc.sync.dma_start(
            out=bias_rows[F_TILES : F_TILES + E_TILES, :],
            in_=mlp_b2.rearrange("(a p) -> a p", p=P),
        )
        nc.sync.dma_start(out=shift_row[0:1, :], in_=ln3_b.rearrange("(o e) -> o e", o=1))
        for cols in halves:
            for u in range(2):
                nc.sync.dma_start(
                    out=w1_raw[:, 2 * u : 2 * u + 2, cols],
                    in_=mlp_w1[256 * u : 256 * (u + 1), cols].rearrange("(q e) f -> q e f", e=2),
                )
        nc.sync.dma_start(out=x_sb[1][:], in_=x_rows[1])
        nc.sync.dma_start(out=w2_raw[:], in_=mlp_w2.rearrange("(a p) e -> p a e", p=P))
        for g in range(2, N_GROUPS):
            nc.sync.dma_start(out=x_sb[g][:], in_=x_rows[g])
            if g == 3:
                nc.sync.dma_start(out=gain[:], in_=ln3_g.partition_broadcast(P))

        ident_f32 = keep.tile([P, P], F32)
        make_identity(nc, ident_f32[:])
        ident_bf16 = keep.tile([P, P], BF16)
        make_identity(nc, ident_bf16[:])
        ones = keep.tile([P, P], BF16)
        nc.vector.memset(ones[:], 1.0)
        eps = keep.tile([P, 1], F32)
        nc.vector.memset(eps[:], EPS)
        table_warm = keep.tile([P, 1], F32)
        nc.scalar.activation(out=table_warm[:], in_=eps[:], func=ACT.Abs_reciprocal_sqrt)

        w1_grouped = keep.tile([P, F, PACK], BF16, align_bytes=64)
        w1_codes = keep.tile([P, F], U32, align_bytes=64)
        w1_scales = keep.tile([P, F], U8, align_bytes=64)
        w2_grouped = keep.tile([P, PASSES2, E, PACK], BF16, align_bytes=64)
        w2_codes = keep.tile([P, PASSES2, E], U32, align_bytes=64)
        w2_scales = keep.tile([P, PASSES2, E], U8, align_bytes=64)
        bias_cols = keep.tile([P, F_TILES + E_TILES], F32)
        shift_ps = psum.tile([P, E], F32, tag="shift_ps")

        x_grouped, x_codes, x_scales = {}, {}, {}
        h_planes, h_grouped, h_codes, h_scales = {}, {}, {}, {}
        m_relu, y_ps, stats, mean_var, centred_gain, rstd = {}, {}, {}, {}, {}, {}

        free_banks = list(range(BANKS))
        held_banks = []

        def next_bank(hold):
            for entry in held_banks:
                entry[0] -= 1
            while held_banks and held_banks[0][0] == 0:
                free_banks.append(held_banks.pop(0)[1])
            bank = free_banks.pop(0)
            if hold:
                held_banks.append([hold, bank])
            else:
                free_banks.append(bank)
            return "bank%d" % bank

        def exists(g):
            return 0 <= g < N_GROUPS

        def transpose_x(g, half):
            if not exists(g):
                return
            if half == 0:
                x_grouped[g] = work.tile([P, GROUP, PACK], BF16, name="x_grouped", align_bytes=64)
            x_words = (
                x_grouped[g][:]
                .rearrange("p c t -> p (c t)")
                .bitcast(F32)
                .rearrange("p (c u) -> p c u", u=2)
            )
            xt = psum.tile([P, 2, 2 * P], F32, tag=next_bank(0))
            for jj in range(2):
                words = x_sb[g][:, 2 * half + jj, :].bitcast(F32)
                for u in range(2):
                    nc.tensor.transpose(
                        xt[:, u, jj * P : (jj + 1) * P], words[:, u * P : (u + 1) * P], ident_f32[:]
                    )
            nc.scalar.copy(
                out=x_words[:, half * 2 * P : (half + 1) * 2 * P, :],
                in_=xt[:].rearrange("p u c -> p c u"),
            )

        def quantise_x(g):
            if not exists(g):
                return
            x_codes[g] = work.tile([P, GROUP], U32, name="x_codes", bufs=3, align_bytes=64)
            x_scales[g] = work.tile([P, GROUP], U8, name="x_scales", bufs=3, align_bytes=64)
            quantise(nc, x_codes[g][:], x_scales[g][:], x_grouped[g][:])

        def first_matmul(g, a):
            if not exists(g):
                return
            c, t = divmod(a, PACK)
            if t == 0:
                h_planes[g, c] = work.tile([P, PACK, GROUP], BF16, name="h_planes", bufs=4)
            h_ps = psum.tile([P, GROUP], F32, tag=next_bank(0))
            nc.tensor.matmul_mx(
                out=h_ps[:],
                lhsT=w1_codes[:, a * P : (a + 1) * P].bitcast(FP8X4),
                lhsT_scale=w1_scales[:, a * P : (a + 1) * P],
                rhs=x_codes[g][:].bitcast(FP8X4),
                rhs_scale=x_scales[g][:],
                start=True,
                stop=True,
            )
            if (g, a) == (1, 7):
                nc.vector.tensor_scalar(
                    out=h_planes[g, c][:, t, :],
                    in0=h_ps[:],
                    scalar1=bias_cols[:, a : a + 1],
                    scalar2=0.0,
                    op0=ALU.add,
                    op1=ALU.max,
                )
                return
            nc.scalar.activation(
                out=h_planes[g, c][:, t, :],
                in_=h_ps[:],
                func=ACT.Relu,
                bias=bias_cols[:, a : a + 1],
                scale=1.0,
            )

        def interleave_h(g, c):
            if not exists(g):
                return
            if c == 0:
                h_grouped[g] = work.tile(
                    [P, PASSES2, GROUP, PACK], BF16, name="h_grouped", align_bytes=64
                )
            if g < 2:
                interleave(nc, h_grouped[g][:, c, :, :], h_planes[g, c][:])
            else:
                interleave_beside_vector(nc, h_grouped[g][:, c, :, :], h_planes[g, c][:])

        def quantise_h(g, c):
            if not exists(g):
                return
            if c == 0:
                h_codes[g] = work.tile([P, PASSES2, GROUP], U32, name="h_codes", align_bytes=64)
                h_scales[g] = work.tile([P, PASSES2, GROUP], U8, name="h_scales", align_bytes=64)
            quantise(nc, h_codes[g][:, c, :], h_scales[g][:, c, :], h_grouped[g][:, c, :, :])

        def second_matmul(g, a):
            if not exists(g):
                return
            if a == 0:
                m_relu[g] = work.tile([P, E_TILES, GROUP], F32, name="m_relu")
            m_ps = psum.tile([P, GROUP], F32, tag=next_bank(0))
            for c in range(PASSES2):
                nc.tensor.matmul_mx(
                    out=m_ps[:],
                    lhsT=w2_codes[:, c, a * P : (a + 1) * P].bitcast(FP8X4),
                    lhsT_scale=w2_scales[:, c, a * P : (a + 1) * P],
                    rhs=h_codes[g][:, c, :].bitcast(FP8X4),
                    rhs_scale=h_scales[g][:, c, :],
                    start=(c == 0),
                    stop=(c == PASSES2 - 1),
                )
            nc.scalar.activation(
                out=m_relu[g][:, a, :],
                in_=m_ps[:],
                func=ACT.Relu,
                bias=bias_cols[:, F_TILES + a : F_TILES + a + 1],
                scale=1.0,
            )

        def assemble_y(g, tiles):
            if not exists(g):
                return
            for j in tiles:
                y_ps[g, j] = psum.tile([P, E], F32, name="y_ps", tag=next_bank(HELD))
                nc.tensor.matmul(
                    out=y_ps[g, j][:], lhsT=ident_bf16[:], rhs=x_sb[g][:, j, :], start=True, stop=False
                )
            for j in tiles:
                for a in range(E_TILES):
                    nc.tensor.matmul(
                        out=y_ps[g, j][:, a * P : (a + 1) * P],
                        lhsT=m_relu[g][:, a, j * P : (j + 1) * P],
                        rhs=ident_f32[:],
                        is_transpose=True,
                        start=False,
                        stop=(a == E_TILES - 1),
                    )

        def tile_statistics(g, j):
            if not exists(g):
                return
            if j == 0:
                stats[g] = work.tile([P, TILES, 6], F32, name="stats")
                mean_var[g] = work.tile([P, TILES, 2], F32, name="mean_var")
            if on_scalar(g, j):
                statistics_on_scalar(g, j)
            else:
                nc.vector.bn_stats(out=stats[g][:, j, :], in_=y_ps[g, j][:])

        def aggregate(g, j):
            if exists(g) and not on_scalar(g, j):
                nc.vector.bn_aggr(out=mean_var[g][:, j, :], in_=stats[g][:, j, :])

        def on_scalar(g, j):
            return g + 2 >= N_GROUPS and (j % 2 == 1 or (g, j) == (N_GROUPS - 1, 2))

        def statistics_on_scalar(g, j):
            unused = work.tile([P, E], BF16, name="unused")
            nc.scalar.activation(
                out=unused[:],
                in_=y_ps[g, j][:],
                func=ACT.Identity,
                scale=1.0 / E,
                accum_out=mean_var[g][:, j, 0:1],
            )
            unused = work.tile([P, E], BF16, name="unused")
            nc.scalar.activation(
                out=unused[:],
                in_=y_ps[g, j][:],
                func=ACT.Square,
                bias=mean_var[g][:, j, 0:1],
                scale=-1.0,
                accum_out=mean_var[g][:, j, 1:2],
            )

        def centre_and_gain(g, j):
            if not exists(g):
                return
            if g not in centred_gain:
                centred_gain[g] = work.tile([P, TILES, E], F32, name="centred_gain")
            nc.vector.scalar_tensor_tensor(
                out=centred_gain[g][:, j, :],
                in0=y_ps[g, j][:],
                scalar=mean_var[g][:, j, 0:1],
                in1=gain[:],
                op0=ALU.subtract,
                op1=ALU.mult,
            )

        def inverse_std(g, tiles):
            if not exists(g):
                return
            if g not in rstd:
                rstd[g] = work.tile([P, TILES], F32, name="rstd")
            for kind in (False, True):
                of_kind = [j for j in tiles if on_scalar(g, j) == kind]
                if of_kind:
                    part = slice(of_kind[0], of_kind[-1] + 1, of_kind[1] - of_kind[0] if len(of_kind) > 1 else 1)
                    nc.scalar.activation(
                        out=rstd[g][:, part],
                        in_=mean_var[g][:, part, 1],
                        func=ACT.Abs_reciprocal_sqrt,
                        bias=eps[:],
                        scale=1.0 / E if kind else 1.0,
                    )

        def scale_shift_store(g, j):
            if not exists(g):
                return
            result = work.tile([P, E], F32, bufs=4)
            nc.vector.scalar_tensor_tensor(
                out=result[:],
                in0=centred_gain[g][:, j, :],
                scalar=rstd[g][:, j : j + 1],
                in1=shift_ps[:],
                op0=ALU.mult,
                op1=ALU.add,
            )
            nc.sync.dma_start(out=out_rows[g][:, j, :], in_=result[:])

        transpose_x(0, 0)
        transpose_x(0, 1)
        bias_ps = psum.tile([P, P], BF16, tag=next_bank(0))
        nc.tensor.transpose(bias_ps[:], bias_rows[:], ident_bf16[:])
        nc.vector.tensor_copy(out=bias_cols[:], in_=bias_ps[:, 0 : F_TILES + E_TILES])
        nc.tensor.matmul(out=shift_ps[:], lhsT=ones[:], rhs=shift_row[:], start=True, stop=True)
        transpose_x(1, 0)
        transpose_x(1, 1)

        interleave(nc, w1_grouped[:, halves[0], :], w1_raw[:, :, halves[0]])
        quantise_x(0)
        quantise(nc, w1_codes[:, halves[0]], w1_scales[:, halves[0]], w1_grouped[:, halves[0], :])
        interleave(nc, w1_grouped[:, halves[1], :], w1_raw[:, :, halves[1]])
        quantise(nc, w1_codes[:, halves[1]], w1_scales[:, halves[1]], w1_grouped[:, halves[1], :])
        quantise_x(1)
        for c in range(PASSES2):
            interleave(nc, w2_grouped[:, c, :, :], w2_raw[:, c * PACK : (c + 1) * PACK, :])
        for c in range(PASSES2):
            quantise(nc, w2_codes[:, c, :], w2_scales[:, c, :], w2_grouped[:, c, :, :])

        for f in range(-2, N_GROUPS - 2):
            for a in range(E_TILES):
                second_matmul(f, a)
                if a == 0 and exists(f) and f > 0:
                    inverse_std(f - 1, range(TILES))
            scale_shift_store(f - 1, 0)
            scale_shift_store(f - 1, 1)
            quantise_h(f + 1, 0)
            if f >= 1:
                quantise_x(f + 3)
            if f != 0:
                quantise_h(f + 1, 1)
            if f < 1 and f + 3 > 1:
                quantise_x(f + 3)
            for c in range(PASSES2):
                pair = (2 * c, 2 * c + 1)
                if c == 0:
                    for t in range(PACK):
                        first_matmul(f + 2, t)
                    interleave_h(f + 2, c)
                    assemble_y(f, pair)
                else:
                    for t in range(PACK):
                        first_matmul(f + 2, PACK + t)
                    interleave_h(f + 2, c)
                    assemble_y(f, pair)
                    transpose_x(f + 4, 0)
                    transpose_x(f + 4, 1)
                tile_statistics(f, pair[0])
                tile_statistics(f, pair[1])
                aggregate(f, pair[0])
                if f == 0 and c == 0:
                    quantise_h(f + 1, 1)
                else:
                    scale_shift_store(f - 1, 2 + c)
                aggregate(f, pair[1])
                centre_and_gain(f, pair[0])
                centre_and_gain(f, pair[1])

        p, q = N_GROUPS - 2, N_GROUPS - 1
        second_matmul(p, 0)
        second_matmul(p, 1)
        inverse_std(p - 1, range(TILES))
        second_matmul(p, 2)
        second_matmul(p, 3)
        scale_shift_store(p - 1, 0)
        scale_shift_store(p - 1, 1)
        assemble_y(p, (0, 1))
        tile_statistics(p, 0)
        quantise_h(q, 0)
        quantise_h(q, 1)
        assemble_y(p, (2, 3))
        tile_statistics(p, 1)
        tile_statistics(p, 3)
        aggregate(p, 0)
        for a in range(3):
            second_matmul(q, a)
        tile_statistics(p, 2)
        scale_shift_store(p - 1, 2)
        centre_and_gain(p, 0)
        centre_and_gain(p, 1)
        aggregate(p, 2)
        scale_shift_store(p - 1, 3)
        centre_and_gain(p, 2)
        centre_and_gain(p, 3)
        inverse_std(p, range(TILES))
        second_matmul(q, 3)
        scale_shift_store(p, 0)
        scale_shift_store(p, 1)
        assemble_y(q, (0, 1))
        tile_statistics(q, 0)
        tile_statistics(q, 1)
        scale_shift_store(p, 2)
        aggregate(q, 0)
        assemble_y(q, (2, 3))
        tile_statistics(q, 2)
        inverse_std(q, (0, 1))
        tile_statistics(q, 3)
        scale_shift_store(p, 3)
        centre_and_gain(q, 0)
        centre_and_gain(q, 1)
        scale_shift_store(q, 0)
        scale_shift_store(q, 1)
        centre_and_gain(q, 2)
        inverse_std(q, (2,))
        centre_and_gain(q, 3)
        inverse_std(q, (3,))
        scale_shift_store(q, 2)
        scale_shift_store(q, 3)
